import numpy as np
import ml_dtypes

BF16 = ml_dtypes.bfloat16


def bf(x):
    return np.asarray(x, np.float32).astype(BF16)


def f32(x):
    return np.asarray(x, np.float32)


def f64(x):
    return np.asarray(x).astype(np.float64)


def striped(idx):
    return np.tile(idx.reshape(-1, 16).T, (8, 1))


C, S, N = 128, 512, 128
EPS = 1e-6


def pos_table():
    div = np.exp(f32(np.arange(0, N, 2)) * np.float32(-np.log(10000.0) / N))
    ang = f32(np.arange(C))[:, None] * div[None, :]
    pe = np.zeros((C, N), np.float32)
    pe[:, 0::2] = np.sin(ang)
    pe[:, 1::2] = np.cos(ang)
    return pe


def setup_inputs():
    return {"base": f32(np.random.standard_normal((C, S))), "src": f32(0.1 * np.random.standard_normal((C, N))), "pe": f32(pos_table()), "gain": f32(1.0 + 0.1 * np.random.standard_normal((1, N))), "bias": f32(0.1 * np.random.standard_normal((1, N))), "offs": striped(np.random.permutation(S)[:N])}


def reference(base, src, pe, gain, bias, offs):
    idx = offs[:16].T.reshape(-1)
    h = f64(src) * np.sqrt(N) + f64(pe)
    m = h.mean(axis=1, keepdims=True)
    var = ((h - m) ** 2).mean(axis=1, keepdims=True)
    out = f64(base).copy()
    out[:, idx] = (h - m) / np.sqrt(var + EPS) * f64(gain) + f64(bias)
    return out

@@ -1,0 +1,59 @@
+import math
+
+import concourse.mybir as mybir
+
+F32 = mybir.dt.float32
+U16 = mybir.dt.uint16
+ALU = mybir.AluOpType
+FUNC = mybir.ActivationFunctionType
+
+TOKENS = 128
+FEATURES = 128
+COLUMNS = 512
+EPS = 1e-6
+BN_STATS_DIM = 6
+BN_AGGR_DIM = 2
+
+
+def tile_rxng2sequencer_kernel(tc, base, src, pe, gain, bias, offs, out):
+    nc = tc.nc
+    with tc.tile_pool(name="held", bufs=1) as held:
+        src_sb = held.tile([TOKENS, FEATURES], F32, name="src_sb")
+        nc.sync.dma_start(src_sb[:], src)
+        pe_sb = held.tile([TOKENS, FEATURES], F32, name="pe_sb")
+        nc.scalar.dma_start(pe_sb[:], pe)
+        offsets = held.tile([TOKENS, FEATURES // 16], U16, name="offsets")
+        nc.sync.dma_start(offsets[:], offs)
+        gain_sb = held.tile([TOKENS, FEATURES], F32, name="gain_sb")
+        nc.scalar.dma_start(gain_sb[:], gain.broadcast_to([TOKENS, FEATURES]))
+        bias_sb = held.tile([TOKENS, FEATURES], F32, name="bias_sb")
+        nc.scalar.dma_start(bias_sb[:], bias.broadcast_to([TOKENS, FEATURES]))
+        window = held.tile([TOKENS, COLUMNS], F32, name="window")
+        nc.sync.dma_start(window[:], base)
+
+        eps_sb = held.tile([TOKENS, 1], F32, name="eps_sb")
+        nc.vector.memset(eps_sb[:], EPS)
+
+        h = held.tile([TOKENS, FEATURES], F32, name="h")
+        nc.vector.scalar_tensor_tensor(h[:], src_sb[:], math.sqrt(FEATURES), pe_sb[:], ALU.mult, ALU.add)
+
+        stats = held.tile([TOKENS, BN_STATS_DIM], F32, name="stats")
+        nc.vector.bn_stats(stats[:], h[:])
+        mean_var = held.tile([TOKENS, BN_AGGR_DIM], F32, name="mean_var")
+        nc.vector.bn_aggr(mean_var[:], stats[:])
+        mean = mean_var[:, 0:1]
+        var = mean_var[:, 1:2]
+
+        std = held.tile([TOKENS, 1], F32, name="std")
+        nc.scalar.activation(std[:], var, FUNC.Sqrt, bias=eps_sb[:])
+        rstd = held.tile([TOKENS, 1], F32, name="rstd")
+        nc.vector.reciprocal(rstd[:], std[:])
+
+        centred = held.tile([TOKENS, FEATURES], F32, name="centred")
+        nc.vector.scalar_tensor_tensor(centred[:], h[:], mean, gain_sb[:], ALU.subtract, ALU.mult)
+        scaled = held.tile([TOKENS, FEATURES], F32, name="scaled")
+        nc.vector.tensor_scalar(scaled[:], centred[:], rstd[:], None, ALU.mult)
+
+        nc.vector.tensor_tensor(window[:].indirect(offsets[:]), scaled[:], bias_sb[:], ALU.add)
+
+        nc.sync.dma_start(out, window[:])

@@ -13,26 +13,33 @@ COLUMNS = 512
 EPS = 1e-6
 BN_STATS_DIM = 6
 BN_AGGR_DIM = 2
+ROWS = 32
 
 
 def tile_rxng2sequencer_kernel(tc, base, src, pe, gain, bias, offs, out):
     nc = tc.nc
-    with tc.tile_pool(name="held", bufs=1) as held:
+    with tc.tile_pool(name="held", bufs=1) as held, tc.psum_pool(name="psum", bufs=1) as psum:
         src_sb = held.tile([TOKENS, FEATURES], F32, name="src_sb")
         nc.sync.dma_start(src_sb[:], src)
         pe_sb = held.tile([TOKENS, FEATURES], F32, name="pe_sb")
         nc.scalar.dma_start(pe_sb[:], pe)
+        gain_bias = held.tile([ROWS, 2 * FEATURES], F32, name="gain_bias")
+        nc.sync.dma_start(gain_bias[:, 0:FEATURES], gain.broadcast_to([ROWS, FEATURES]))
+        nc.sync.dma_start(gain_bias[:, FEATURES : 2 * FEATURES], bias.broadcast_to([ROWS, FEATURES]))
         offsets = held.tile([TOKENS, FEATURES // 16], U16, name="offsets")
         nc.sync.dma_start(offsets[:], offs)
-        gain_sb = held.tile([TOKENS, FEATURES], F32, name="gain_sb")
-        nc.scalar.dma_start(gain_sb[:], gain.broadcast_to([TOKENS, FEATURES]))
-        bias_sb = held.tile([TOKENS, FEATURES], F32, name="bias_sb")
-        nc.scalar.dma_start(bias_sb[:], bias.broadcast_to([TOKENS, FEATURES]))
         window = held.tile([TOKENS, COLUMNS], F32, name="window")
         nc.sync.dma_start(window[:], base)
 
         eps_sb = held.tile([TOKENS, 1], F32, name="eps_sb")
         nc.vector.memset(eps_sb[:], EPS)
+
+        pick_first = held.tile([ROWS, TOKENS], F32, name="pick_first")
+        nc.gpsimd.memset(pick_first[:], 0.0)
+        nc.gpsimd.memset(pick_first[0:1, :], 1.0)
+        spread = psum.tile([TOKENS, 2 * FEATURES], F32, name="spread")
+        nc.tensor.matmul(spread[:], pick_first[:], gain_bias[:], start=True, stop=True)
+        gain_ps = spread[:, 0:FEATURES]
 
         h = held.tile([TOKENS, FEATURES], F32, name="h")
         nc.vector.scalar_tensor_tensor(h[:], src_sb[:], math.sqrt(FEATURES), pe_sb[:], ALU.mult, ALU.add)
@@ -46,11 +53,13 @@ def tile_rxng2sequencer_kernel(tc, base, src, pe, gain, bias, offs, out):
 
         std = held.tile([TOKENS, 1], F32, name="std")
         nc.scalar.activation(std[:], var, FUNC.Sqrt, bias=eps_sb[:])
+        bias_sb = held.tile([TOKENS, FEATURES], F32, name="bias_sb")
+        nc.scalar.copy(bias_sb[:], spread[:, FEATURES : 2 * FEATURES])
         rstd = held.tile([TOKENS, 1], F32, name="rstd")
         nc.vector.reciprocal(rstd[:], std[:])
 
         centred = held.tile([TOKENS, FEATURES], F32, name="centred")
-        nc.vector.scalar_tensor_tensor(centred[:], h[:], mean, gain_sb[:], ALU.subtract, ALU.mult)
+        nc.vector.scalar_tensor_tensor(centred[:], h[:], mean, gain_ps, ALU.subtract, ALU.mult)
         scaled = held.tile([TOKENS, FEATURES], F32, name="scaled")
         nc.vector.tensor_scalar(scaled[:], centred[:], rstd[:], None, ALU.mult)
 

@@ -22,7 +22,7 @@ def tile_rxng2sequencer_kernel(tc, base, src, pe, gain, bias, offs, out):
         src_sb = held.tile([TOKENS, FEATURES], F32, name="src_sb")
         nc.sync.dma_start(src_sb[:], src)
         pe_sb = held.tile([TOKENS, FEATURES], F32, name="pe_sb")
-        nc.scalar.dma_start(pe_sb[:], pe)
+        nc.sync.dma_start(pe_sb[:], pe)
         gain_bias = held.tile([ROWS, 2 * FEATURES], F32, name="gain_bias")
         nc.sync.dma_start(gain_bias[:, 0:FEATURES], gain.broadcast_to([ROWS, FEATURES]))
         nc.sync.dma_start(gain_bias[:, FEATURES : 2 * FEATURES], bias.broadcast_to([ROWS, FEATURES]))

@@ -24,8 +24,9 @@ def tile_rxng2sequencer_kernel(tc, base, src, pe, gain, bias, offs, out):
         pe_sb = held.tile([TOKENS, FEATURES], F32, name="pe_sb")
         nc.sync.dma_start(pe_sb[:], pe)
         gain_bias = held.tile([ROWS, 2 * FEATURES], F32, name="gain_bias")
-        nc.sync.dma_start(gain_bias[:, 0:FEATURES], gain.broadcast_to([ROWS, FEATURES]))
-        nc.sync.dma_start(gain_bias[:, FEATURES : 2 * FEATURES], bias.broadcast_to([ROWS, FEATURES]))
+        nc.vector.memset(gain_bias[:], 0.0)
+        nc.sync.dma_start(gain_bias[0:1, 0:FEATURES], gain)
+        nc.sync.dma_start(gain_bias[0:1, FEATURES : 2 * FEATURES], bias)
         offsets = held.tile([TOKENS, FEATURES // 16], U16, name="offsets")
         nc.sync.dma_start(offsets[:], offs)
         window = held.tile([TOKENS, COLUMNS], F32, name="window")
@@ -34,11 +35,10 @@ def tile_rxng2sequencer_kernel(tc, base, src, pe, gain, bias, offs, out):
         eps_sb = held.tile([TOKENS, 1], F32, name="eps_sb")
         nc.vector.memset(eps_sb[:], EPS)
 
-        pick_first = held.tile([ROWS, TOKENS], F32, name="pick_first")
-        nc.gpsimd.memset(pick_first[:], 0.0)
-        nc.gpsimd.memset(pick_first[0:1, :], 1.0)
+        ones = held.tile([ROWS, TOKENS], F32, name="ones")
+        nc.gpsimd.memset(ones[:], 1.0)
         spread = psum.tile([TOKENS, 2 * FEATURES], F32, name="spread")
-        nc.tensor.matmul(spread[:], pick_first[:], gain_bias[:], start=True, stop=True)
+        nc.tensor.matmul(spread[:], ones[:], gain_bias[:], start=True, stop=True)
         gain_ps = spread[:, 0:FEATURES]
 
         h = held.tile([TOKENS, FEATURES], F32, name="h")

@@ -23,10 +23,12 @@ def tile_rxng2sequencer_kernel(tc, base, src, pe, gain, bias, offs, out):
         nc.sync.dma_start(src_sb[:], src)
         pe_sb = held.tile([TOKENS, FEATURES], F32, name="pe_sb")
         nc.sync.dma_start(pe_sb[:], pe)
-        gain_bias = held.tile([ROWS, 2 * FEATURES], F32, name="gain_bias")
-        nc.vector.memset(gain_bias[:], 0.0)
-        nc.sync.dma_start(gain_bias[0:1, 0:FEATURES], gain)
-        nc.sync.dma_start(gain_bias[0:1, FEATURES : 2 * FEATURES], bias)
+        gain_row = held.tile([ROWS, FEATURES], F32, name="gain_row")
+        nc.vector.memset(gain_row[:], 0.0)
+        nc.sync.dma_start(gain_row[0:1, :], gain)
+        bias_row = held.tile([ROWS, FEATURES], F32, name="bias_row")
+        nc.vector.memset(bias_row[:], 0.0)
+        nc.sync.dma_start(bias_row[0:1, :], bias)
         offsets = held.tile([TOKENS, FEATURES // 16], U16, name="offsets")
         nc.sync.dma_start(offsets[:], offs)
         window = held.tile([TOKENS, COLUMNS], F32, name="window")
@@ -37,9 +39,10 @@ def tile_rxng2sequencer_kernel(tc, base, src, pe, gain, bias, offs, out):
 
         ones = held.tile([ROWS, TOKENS], F32, name="ones")
         nc.gpsimd.memset(ones[:], 1.0)
-        spread = psum.tile([TOKENS, 2 * FEATURES], F32, name="spread")
-        nc.tensor.matmul(spread[:], ones[:], gain_bias[:], start=True, stop=True)
-        gain_ps = spread[:, 0:FEATURES]
+        gain_ps = psum.tile([TOKENS, FEATURES], F32, name="gain_ps")
+        nc.tensor.matmul(gain_ps[:], ones[:], gain_row[:], start=True, stop=True)
+        bias_ps = psum.tile([TOKENS, FEATURES], F32, name="bias_ps")
+        nc.tensor.matmul(bias_ps[:], ones[:], bias_row[:], start=True, stop=True)
 
         h = held.tile([TOKENS, FEATURES], F32, name="h")
         nc.vector.scalar_tensor_tensor(h[:], src_sb[:], math.sqrt(FEATURES), pe_sb[:], ALU.mult, ALU.add)
@@ -53,15 +56,14 @@ def tile_rxng2sequencer_kernel(tc, base, src, pe, gain, bias, offs, out):
 
         std = held.tile([TOKENS, 1], F32, name="std")
         nc.scalar.activation(std[:], var, FUNC.Sqrt, bias=eps_sb[:])
-        bias_sb = held.tile([TOKENS, FEATURES], F32, name="bias_sb")
-        nc.scalar.copy(bias_sb[:], spread[:, FEATURES : 2 * FEATURES])
+        centred = held.tile([TOKENS, FEATURES], F32, name="centred")
+        nc.vector.scalar_tensor_tensor(centred[:], h[:], mean, gain_ps[:], ALU.subtract, ALU.mult)
         rstd = held.tile([TOKENS, 1], F32, name="rstd")
         nc.vector.reciprocal(rstd[:], std[:])
-
-        centred = held.tile([TOKENS, FEATURES], F32, name="centred")
-        nc.vector.scalar_tensor_tensor(centred[:], h[:], mean, gain_ps, ALU.subtract, ALU.mult)
         scaled = held.tile([TOKENS, FEATURES], F32, name="scaled")
         nc.vector.tensor_scalar(scaled[:], centred[:], rstd[:], None, ALU.mult)
+        bias_sb = held.tile([TOKENS, FEATURES], F32, name="bias_sb")
+        nc.vector.tensor_copy(bias_sb[:], bias_ps[:])
 
         nc.vector.tensor_tensor(window[:].indirect(offsets[:]), scaled[:], bias_sb[:], ALU.add)
 

@@ -54,12 +54,10 @@ def tile_rxng2sequencer_kernel(tc, base, src, pe, gain, bias, offs, out):
         mean = mean_var[:, 0:1]
         var = mean_var[:, 1:2]
 
-        std = held.tile([TOKENS, 1], F32, name="std")
-        nc.scalar.activation(std[:], var, FUNC.Sqrt, bias=eps_sb[:])
+        rstd = held.tile([TOKENS, 1], F32, name="rstd")
+        nc.scalar.activation(rstd[:], var, FUNC.Abs_reciprocal_sqrt, bias=eps_sb[:])
         centred = held.tile([TOKENS, FEATURES], F32, name="centred")
         nc.vector.scalar_tensor_tensor(centred[:], h[:], mean, gain_ps[:], ALU.subtract, ALU.mult)
-        rstd = held.tile([TOKENS, 1], F32, name="rstd")
-        nc.vector.reciprocal(rstd[:], std[:])
         scaled = held.tile([TOKENS, FEATURES], F32, name="scaled")
         nc.vector.tensor_scalar(scaled[:], centred[:], rstd[:], None, ALU.mult)
         bias_sb = held.tile([TOKENS, FEATURES], F32, name="bias_sb")

@@ -58,10 +58,10 @@ def tile_rxng2sequencer_kernel(tc, base, src, pe, gain, bias, offs, out):
         nc.scalar.activation(rstd[:], var, FUNC.Abs_reciprocal_sqrt, bias=eps_sb[:])
         centred = held.tile([TOKENS, FEATURES], F32, name="centred")
         nc.vector.scalar_tensor_tensor(centred[:], h[:], mean, gain_ps[:], ALU.subtract, ALU.mult)
-        scaled = held.tile([TOKENS, FEATURES], F32, name="scaled")
-        nc.vector.tensor_scalar(scaled[:], centred[:], rstd[:], None, ALU.mult)
         bias_sb = held.tile([TOKENS, FEATURES], F32, name="bias_sb")
         nc.vector.tensor_copy(bias_sb[:], bias_ps[:])
+        scaled = held.tile([TOKENS, FEATURES], F32, name="scaled")
+        nc.vector.tensor_scalar(scaled[:], centred[:], rstd[:], None, ALU.mult)
 
         nc.vector.tensor_tensor(window[:].indirect(offsets[:]), scaled[:], bias_sb[:], ALU.add)
 

@@ -12,7 +12,6 @@ FEATURES = 128
 COLUMNS = 512
 EPS = 1e-6
 BN_STATS_DIM = 6
-BN_AGGR_DIM = 2
 ROWS = 32
 
 
@@ -48,14 +47,14 @@ def tile_rxng2sequencer_kernel(tc, base, src, pe, gain, bias, offs, out):
         nc.vector.scalar_tensor_tensor(h[:], src_sb[:], math.sqrt(FEATURES), pe_sb[:], ALU.mult, ALU.add)
 
         stats = held.tile([TOKENS, BN_STATS_DIM], F32, name="stats")
-        nc.vector.bn_stats(stats[:], h[:])
-        mean_var = held.tile([TOKENS, BN_AGGR_DIM], F32, name="mean_var")
-        nc.vector.bn_aggr(mean_var[:], stats[:])
-        mean = mean_var[:, 0:1]
-        var = mean_var[:, 1:2]
+        nc.vector.bn_stats(stats[:], h[:].unsqueeze(2).broadcast_to([TOKENS, FEATURES, 2]))
+        mean = stats[:, 1:2]
+        var_times_count = stats[:, 2:3]
 
         rstd = held.tile([TOKENS, 1], F32, name="rstd")
-        nc.scalar.activation(rstd[:], var, FUNC.Abs_reciprocal_sqrt, bias=eps_sb[:])
+        nc.scalar.activation(
+            rstd[:], var_times_count, FUNC.Abs_reciprocal_sqrt, bias=eps_sb[:], scale=1.0 / FEATURES
+        )
         centred = held.tile([TOKENS, FEATURES], F32, name="centred")
         nc.vector.scalar_tensor_tensor(centred[:], h[:], mean, gain_ps[:], ALU.subtract, ALU.mult)
         bias_sb = held.tile([TOKENS, FEATURES], F32, name="bias_sb")

import math

import concourse.mybir as mybir

F32 = mybir.dt.float32
U16 = mybir.dt.uint16
ALU = mybir.AluOpType
FUNC = mybir.ActivationFunctionType

TOKENS = 128
FEATURES = 128
COLUMNS = 512
EPS = 1e-6
BN_STATS_DIM = 6
ROWS = 32


def tile_rxng2sequencer_kernel(tc, base, src, pe, gain, bias, offs, out):
    nc = tc.nc
    with tc.tile_pool(name="held", bufs=1) as held, tc.psum_pool(name="psum", bufs=1) as psum:
        src_sb = held.tile([TOKENS, FEATURES], F32, name="src_sb")
        nc.sync.dma_start(src_sb[:], src)
        pe_sb = held.tile([TOKENS, FEATURES], F32, name="pe_sb")
        nc.sync.dma_start(pe_sb[:], pe)
        gain_row = held.tile([ROWS, FEATURES], F32, name="gain_row")
        nc.vector.memset(gain_row[:], 0.0)
        nc.sync.dma_start(gain_row[0:1, :], gain)
        bias_row = held.tile([ROWS, FEATURES], F32, name="bias_row")
        nc.vector.memset(bias_row[:], 0.0)
        nc.sync.dma_start(bias_row[0:1, :], bias)
        offsets = held.tile([TOKENS, FEATURES // 16], U16, name="offsets")
        nc.sync.dma_start(offsets[:], offs)
        window = held.tile([TOKENS, COLUMNS], F32, name="window")
        nc.sync.dma_start(window[:], base)

        eps_sb = held.tile([TOKENS, 1], F32, name="eps_sb")
        nc.vector.memset(eps_sb[:], EPS)

        ones = held.tile([ROWS, TOKENS], F32, name="ones")
        nc.gpsimd.memset(ones[:], 1.0)
        gain_ps = psum.tile([TOKENS, FEATURES], F32, name="gain_ps")
        nc.tensor.matmul(gain_ps[:], ones[:], gain_row[:], start=True, stop=True)
        bias_ps = psum.tile([TOKENS, FEATURES], F32, name="bias_ps")
        nc.tensor.matmul(bias_ps[:], ones[:], bias_row[:], start=True, stop=True)

        h = held.tile([TOKENS, FEATURES], F32, name="h")
        nc.vector.scalar_tensor_tensor(h[:], src_sb[:], math.sqrt(FEATURES), pe_sb[:], ALU.mult, ALU.add)

        stats = held.tile([TOKENS, BN_STATS_DIM], F32, name="stats")
        nc.vector.bn_stats(stats[:], h[:].unsqueeze(2).broadcast_to([TOKENS, FEATURES, 2]))
        mean = stats[:, 1:2]
        var_times_count = stats[:, 2:3]

        rstd = held.tile([TOKENS, 1], F32, name="rstd")
        nc.scalar.activation(
            rstd[:], var_times_count, FUNC.Abs_reciprocal_sqrt, bias=eps_sb[:], scale=1.0 / FEATURES
        )
        centred = held.tile([TOKENS, FEATURES], F32, name="centred")
        nc.vector.scalar_tensor_tensor(centred[:], h[:], mean, gain_ps[:], ALU.subtract, ALU.mult)
        bias_sb = held.tile([TOKENS, FEATURES], F32, name="bias_sb")
        nc.vector.tensor_copy(bias_sb[:], bias_ps[:])
        scaled = held.tile([TOKENS, FEATURES], F32, name="scaled")
        nc.vector.tensor_scalar(scaled[:], centred[:], rstd[:], None, ALU.mult)

        nc.vector.tensor_tensor(window[:].indirect(offsets[:]), scaled[:], bias_sb[:], ALU.add)

        nc.sync.dma_start(out, window[:])
